import numpy as np
import ml_dtypes


def mxq(x, axis, fmt="e4m3"):
    dtype, down = {"e4m3": (ml_dtypes.float8_e4m3fn, 7), "e5m2": (ml_dtypes.float8_e5m2, 14)}[fmt]
    v = np.moveaxis(np.asarray(x, np.float32).astype(ml_dtypes.bfloat16).astype(np.float64), axis, -1)
    blocks = v.reshape(v.shape[:-1] + (-1, 32))
    amax = np.abs(blocks).max(-1, keepdims=True)
    byte = np.maximum(np.where(amax > 0, np.frexp(amax)[1] - 1 + 127, 0) - down, 1)
    scale = np.exp2(byte - 127.0)
    codes = (blocks / scale).astype(np.float32).astype(dtype).astype(np.float64)
    return np.moveaxis((codes * scale).reshape(v.shape), -1, axis)


WIDE = False


def mx_kscale(k):
    if not WIDE:
        return np.ones(k)
    levels = np.array([10, -10, 5, -5, 0])
    a = np.random.permutation(np.resize(levels, k // 512 * 4)).reshape(k // 512, 4)
    idx = np.arange(k)
    return np.exp2(a[idx // 512, idx % 128 // 32])


BF16 = ml_dtypes.bfloat16


def bf(x):
    return np.asarray(x, np.float32).astype(BF16)


def f64(x):
    return np.asarray(x).astype(np.float64)


B, L, A, W = 128, 512, 1024, 32
EPS = 1e-8


def sigmoid(v):
    return 1.0 / (1.0 + np.exp(-v))


def setup_inputs():
    s, t = mx_kscale(L), mx_kscale(A)
    return {
        "z_current": bf(np.random.standard_normal((B, L)) * s),
        "z_window": bf(np.random.standard_normal((W, B, L)) * s),
        "Wq": bf(np.random.standard_normal((A, L)) / np.sqrt(L) / s),
        "Wk": bf(np.random.standard_normal((A, L)) / np.sqrt(L) / s),
        "Wv": bf(np.random.standard_normal((A, L)) / np.sqrt(L) / s * t[:, None]),
        "Wo": bf(np.random.standard_normal((L, A)) * 2.0 / np.sqrt(A) / t),
    }


def reference(z_current, z_window, Wq, Wk, Wv, Wo):
    sig_q = sigmoid(mxq(f64(z_current), 1, "e4m3") @ mxq(f64(Wq), 1, "e4m3").T)
    zw = mxq(f64(z_window), 2, "e4m3")
    k = zw @ mxq(f64(Wk), 1, "e4m3").T
    v = zw @ mxq(f64(Wv), 1, "e4m3").T
    m = k.max(axis=(1, 2), keepdims=True)
    e = np.exp(k - m)
    num = (e * v).sum(0)
    den = EPS + e.sum(0)
    h = sig_q * (num / den)
    return mxq(h, 1, "e4m3") @ mxq(f64(Wo), 1, "e4m3").T

@@ -1,0 +1,320 @@
+from contextlib import ExitStack
+
+import concourse.mybir as mybir
+from concourse.masks import make_identity
+
+F32 = mybir.dt.float32
+BF16 = mybir.dt.bfloat16
+U32 = mybir.dt.uint32
+U8 = mybir.dt.uint8
+FP8X4 = mybir.dt.float8_e4m3fn_x4
+ACT = mybir.ActivationFunctionType
+ALU = mybir.AluOpType
+AXIS = mybir.AxisListType
+
+P = 128
+B, L, A, STEPS = 128, 512, 1024, 32
+EPS = 1e-8
+PACK = 4
+BANK = 512
+HALVES = A // BANK
+CHUNKS = A // P
+GROUP = 4
+LAG = 8
+JOBS_PER_STEP = 2
+
+FLOPS = 2 * B * L * A + 2 * 2 * STEPS * B * L * A + 2 * B * A * L
+
+
+def transpose_and_quantise(nc, banks, stage, ident, row_tiles, codes, scales):
+    count = len(row_tiles)
+    grouped = stage.tile([P, GROUP * P * PACK], BF16, tag="grouped", align_bytes=64)
+    grouped_words = grouped[:].bitcast(F32)
+    for first in range(0, count, 2):
+        pair = row_tiles[first : first + 2]
+        width = len(pair) * 2 * P
+        turned = banks.tile([P, BANK], F32, tag="work")
+        for r, words in enumerate(pair):
+            for u in range(2):
+                nc.tensor.transpose(
+                    out=turned[:, (2 * r + u) * P : (2 * r + u + 1) * P],
+                    in_=words[:, u * P : (u + 1) * P],
+                    identity=ident[:],
+                )
+        nc.scalar.copy(
+            out=grouped_words[:, first * 2 * P : first * 2 * P + width].rearrange(
+                "p (r c u) -> p r c u", c=P, u=2
+            ),
+            in_=turned[:, 0:width].rearrange("p (r u c) -> p r c u", u=2, c=P),
+        )
+    nc.vector.quantize_mx(
+        out=codes.bitcast(FP8X4), scales=scales, in_=grouped[:, 0 : count * P * PACK]
+    )
+
+
+def tile_aftblock_pa_t_kernel(tc, z_current, z_window, Wq, Wk, Wv, Wo, out):
+    nc = tc.nc
+    with ExitStack() as ctx:
+        const = ctx.enter_context(tc.tile_pool(name="const", bufs=1))
+        raw = ctx.enter_context(tc.tile_pool(name="raw", bufs=1))
+        stage = ctx.enter_context(tc.tile_pool(name="stage", bufs=3))
+        quant = ctx.enter_context(tc.tile_pool(name="quant", bufs=1))
+        small = ctx.enter_context(tc.tile_pool(name="small", bufs=4))
+        e_pool = ctx.enter_context(tc.tile_pool(name="e_pool", bufs=LAG + 2))
+        prod_pool = ctx.enter_context(tc.tile_pool(name="prod_pool", bufs=3))
+        tail = ctx.enter_context(tc.tile_pool(name="tail", bufs=1))
+        sum_banks = ctx.enter_context(tc.psum_pool(name="sum_banks", bufs=1))
+        key_banks = ctx.enter_context(tc.psum_pool(name="key_banks", bufs=4))
+        work_banks = ctx.enter_context(tc.psum_pool(name="work_banks", bufs=2))
+
+        ident = const.tile([P, P], F32, name="ident")
+        make_identity(nc, ident[:])
+        den = const.tile([P, A], F32, name="den")
+        nc.vector.memset(den[:], EPS)
+
+        ctx.enter_context(tc.manual_schedule())
+
+        wk_raw = raw.tile([P, 4, 2 * L], BF16, name="wk_raw")
+        wv_raw = raw.tile([P, 4, 2 * L], BF16, name="wv_raw")
+        wq_raw = raw.tile([P, 4, 2 * L], BF16, name="wq_raw")
+        wo_raw = raw.tile([P, L // P, A], BF16, name="wo_raw")
+        zc_raw = raw.tile([P, L], BF16, name="zc_raw")
+        z_raw = [raw.tile([P, GROUP, L], BF16, name="z_raw%d" % n) for n in range(STEPS // GROUP)]
+
+        def load_weight(tile_ap, weight):
+            nc.sync.dma_start(
+                out=tile_ap[:], in_=weight.rearrange("(m j e) l -> j m (e l)", m=4, e=2)
+            )
+
+        def load_steps(n):
+            nc.sync.dma_start(
+                out=z_raw[n][:],
+                in_=z_window[n * GROUP : (n + 1) * GROUP].rearrange("w b l -> b w l"),
+            )
+
+        load_weight(wk_raw, Wk)
+        load_steps(0)
+        load_steps(1)
+        load_steps(2)
+        load_weight(wv_raw, Wv)
+        for n in range(3, STEPS // GROUP):
+            load_steps(n)
+        load_weight(wq_raw, Wq)
+        nc.sync.dma_start(out=zc_raw[:], in_=z_current)
+        nc.sync.dma_start(out=wo_raw[:], in_=Wo.rearrange("(c p) a -> p c a", p=P))
+
+        z_codes = quant.tile([P, STEPS * B], U32, name="z_codes", align_bytes=64)
+        z_scales = quant.tile([P, STEPS * B], U8, name="z_scales", align_bytes=64)
+        zc_codes = quant.tile([P, B], U32, name="zc_codes", align_bytes=64)
+        zc_scales = quant.tile([P, B], U8, name="zc_scales", align_bytes=64)
+        wk_codes = quant.tile([P, A], U32, name="wk_codes", align_bytes=64)
+        wk_scales = quant.tile([P, A], U8, name="wk_scales", align_bytes=64)
+        wv_codes = quant.tile([P, A], U32, name="wv_codes", align_bytes=64)
+        wv_scales = quant.tile([P, A], U8, name="wv_scales", align_bytes=64)
+        wq_codes = quant.tile([P, A], U32, name="wq_codes", align_bytes=64)
+        wq_scales = quant.tile([P, A], U8, name="wq_scales", align_bytes=64)
+        wo_codes = quant.tile([P, 2 * L], U32, name="wo_codes", align_bytes=64)
+        wo_scales = quant.tile([P, 2 * L], U8, name="wo_scales", align_bytes=64)
+
+        def weight_job(raw_tile, codes, scales, g):
+            words = raw_tile[:].bitcast(F32)
+            rows = [
+                words[:, 2 * g + u, e * (L // 2) : (e + 1) * (L // 2)]
+                for u in range(2)
+                for e in range(2)
+            ]
+            cols = slice(g * BANK, (g + 1) * BANK)
+            return (rows, codes[:, cols], scales[:, cols])
+
+        def steps_job(n):
+            words = z_raw[n][:].bitcast(F32)
+            cols = slice(n * GROUP * B, (n + 1) * GROUP * B)
+            return ([words[:, s, :] for s in range(GROUP)], z_codes[:, cols], z_scales[:, cols])
+
+        def output_weight_job(g):
+            words = wo_raw[:].bitcast(F32)
+            rows = [words[:, c, g * (BANK // 2) : (g + 1) * (BANK // 2)] for c in range(L // P)]
+            cols = slice(g * L, (g + 1) * L)
+            return (rows, wo_codes[:, cols], wo_scales[:, cols])
+
+        def prepare(job):
+            transpose_and_quantise(nc, work_banks, stage, ident, job[0], job[1], job[2])
+
+        prepare(weight_job(wk_raw, wk_codes, wk_scales, 0))
+        prepare(steps_job(0))
+        prepare(weight_job(wk_raw, wk_codes, wk_scales, 1))
+        jobs = [steps_job(1), steps_job(2)]
+        jobs.extend([weight_job(wv_raw, wv_codes, wv_scales, g) for g in range(2)])
+        jobs.extend([steps_job(n) for n in range(3, STEPS // GROUP)])
+        jobs.extend([weight_job(wq_raw, wq_codes, wq_scales, g) for g in range(2)])
+        jobs.append(([zc_raw[:].bitcast(F32)], zc_codes[:], zc_scales[:]))
+        jobs.extend([output_weight_job(g) for g in range(2)])
+
+        num_t = [sum_banks.tile([P, BANK], F32, name="num_t%d" % g) for g in range(HALVES)]
+
+        k_banks, v_banks, row_maxes, spreads, neg_maxes, e_tiles, prod_tiles = {}, {}, {}, {}, {}, {}, {}
+
+        def step_matmul(banks, tag, w, codes, scales):
+            step = slice(w * B, (w + 1) * B)
+            made = []
+            for h in range(HALVES):
+                cols = slice(h * BANK, (h + 1) * BANK)
+                bank = banks.tile([P, BANK], F32, tag=tag, name="bank_" + tag)
+                nc.tensor.matmul_mx(
+                    out=bank[:],
+                    lhsT=z_codes[:, step].bitcast(FP8X4),
+                    lhsT_scale=z_scales[:, step],
+                    rhs=codes[:, cols].bitcast(FP8X4),
+                    rhs_scale=scales[:, cols],
+                    start=True,
+                    stop=True,
+                )
+                made.append(bank)
+            return made
+
+        def row_maxima(w):
+            half_max = small.tile([P, HALVES], F32, tag="half_max")
+            for h in range(HALVES):
+                nc.vector.reduce_max(out=half_max[:, h : h + 1], in_=k_banks[w][h][:], axis=AXIS.X)
+            row_max = small.tile([P, 1], F32, tag="row_max")
+            nc.vector.reduce_max(out=row_max[:], in_=half_max[:], axis=AXIS.X)
+            row_maxes[w] = row_max
+
+        def spread_maxima(w):
+            spread = work_banks.tile([P, BANK], F32, tag="work")
+            nc.tensor.transpose(
+                out=spread[:, 0:P],
+                in_=row_maxes[w][:, 0:1].to_broadcast([P, P]),
+                identity=ident[:],
+            )
+            spreads[w] = spread
+
+        def step_maximum(w):
+            neg_max = small.tile([P, 1], F32, tag="neg_max")
+            nc.vector.tensor_reduce(
+                out=neg_max[:], in_=spreads[w][:, 0:P], axis=AXIS.X, op=ALU.max, negate=True
+            )
+            neg_maxes[w] = neg_max
+
+        def exponentials(w):
+            e = e_pool.tile([P, A], F32, tag="e")
+            for h in range(HALVES):
+                nc.scalar.activation(
+                    out=e[:, h * BANK : (h + 1) * BANK],
+                    in_=k_banks[w][h][:],
+                    func=ACT.Exp,
+                    bias=neg_maxes[w][:, 0:1],
+                    scale=1.0,
+                )
+            nc.gpsimd.tensor_tensor(out=den[:], in0=den[:], in1=e[:], op=ALU.add)
+            e_tiles[w] = e
+
+        def products(w):
+            prod = prod_pool.tile([P, A], F32, tag="prod")
+            for h in range(HALVES):
+                cols = slice(h * BANK, (h + 1) * BANK)
+                nc.vector.tensor_tensor(
+                    out=prod[:, cols], in0=v_banks[w][h][:], in1=e_tiles[w][:, cols], op=ALU.mult
+                )
+            prod_tiles[w] = prod
+
+        def sum_products(w):
+            for c in range(CHUNKS):
+                g, t = c // PACK, c % PACK
+                nc.tensor.matmul(
+                    out=num_t[g][:, t * B : (t + 1) * B],
+                    lhsT=prod_tiles[w][:, c * P : (c + 1) * P],
+                    rhs=ident[:],
+                    is_transpose=True,
+                    start=(w == 0 and t == 0),
+                    stop=(w == STEPS - 1 and t == PACK - 1),
+                )
+
+        gate_t = tail.tile([P, A], F32, name="gate_t")
+        rec_t = tail.tile([P, A], F32, name="rec_t")
+        scale_t = tail.tile([P, A], F32, name="scale_t")
+
+        def gate():
+            for g in range(HALVES):
+                q_t = key_banks.tile([P, BANK], F32, tag="keys", name="q_t")
+                for t in range(PACK):
+                    c = g * PACK + t
+                    nc.tensor.matmul_mx(
+                        out=q_t[:, t * B : (t + 1) * B],
+                        lhsT=wq_codes[:, c * P : (c + 1) * P].bitcast(FP8X4),
+                        lhsT_scale=wq_scales[:, c * P : (c + 1) * P],
+                        rhs=zc_codes[:].bitcast(FP8X4),
+                        rhs_scale=zc_scales[:],
+                        start=True,
+                        stop=True,
+                    )
+                nc.scalar.activation(
+                    out=gate_t[:, g * BANK : (g + 1) * BANK], in_=q_t[:], func=ACT.Sigmoid
+                )
+
+        def gate_over_denominator():
+            for g in range(HALVES):
+                cols = slice(g * BANK, (g + 1) * BANK)
+                den_t = key_banks.tile([P, BANK], F32, tag="keys", name="den_t")
+                for t in range(PACK):
+                    c = g * PACK + t
+                    nc.tensor.transpose(
+                        out=den_t[:, t * B : (t + 1) * B],
+                        in_=den[:, c * P : (c + 1) * P],
+                        identity=ident[:],
+                    )
+                nc.vector.reciprocal(out=rec_t[:, cols], in_=den_t[:])
+                nc.gpsimd.tensor_tensor(
+                    out=scale_t[:, cols], in0=rec_t[:, cols], in1=gate_t[:, cols], op=ALU.mult
+                )
+
+        k_banks[0] = step_matmul(key_banks, "keys", 0, wk_codes, wk_scales)
+        for i in range(STEPS + LAG + 1):
+            j = i - LAG
+            if 0 <= j < STEPS:
+                v_banks[j] = step_matmul(work_banks, "work", j, wv_codes, wv_scales)
+            if i + 1 < STEPS:
+                k_banks[i + 1] = step_matmul(key_banks, "keys", i + 1, wk_codes, wk_scales)
+            if i == STEPS:
+                gate()
+            if i < STEPS:
+                row_maxima(i)
+            if 0 <= j - 1:
+                sum_products(j - 1)
+            if 0 <= j < STEPS:
+                products(j)
+            if i < STEPS:
+                spread_maxima(i)
+                step_maximum(i)
+                exponentials(i)
+            if i == STEPS + 1:
+                gate_over_denominator()
+            for job in jobs[i * JOBS_PER_STEP : (i + 1) * JOBS_PER_STEP]:
+                prepare(job)
+
+        h_grouped = tail.tile([P, HALVES * B * PACK], BF16, name="h_grouped", align_bytes=64)
+        h_codes = tail.tile([P, HALVES * B], U32, name="h_codes", align_bytes=64)
+        h_scales = tail.tile([P, HALVES * B], U8, name="h_scales", align_bytes=64)
+        for g in range(HALVES):
+            cols = slice(g * BANK, (g + 1) * BANK)
+            nc.vector.tensor_tensor(
+                out=h_grouped[:, cols].rearrange("p (b t) -> p b t", t=PACK),
+                in0=num_t[g][:].rearrange("p (t b) -> p b t", t=PACK),
+                in1=scale_t[:, cols].rearrange("p (t b) -> p b t", t=PACK),
+                op=ALU.mult,
+            )
+        nc.vector.quantize_mx(out=h_codes[:].bitcast(FP8X4), scales=h_scales[:], in_=h_grouped[:])
+        out_bank = work_banks.tile([P, BANK], F32, tag="work")
+        for g in range(HALVES):
+            nc.tensor.matmul_mx(
+                out=out_bank[:],
+                lhsT=h_codes[:, g * B : (g + 1) * B].bitcast(FP8X4),
+                lhsT_scale=h_scales[:, g * B : (g + 1) * B],
+                rhs=wo_codes[:, g * L : (g + 1) * L].bitcast(FP8X4),
+                rhs_scale=wo_scales[:, g * L : (g + 1) * L],
+                start=(g == 0),
+                stop=(g == HALVES - 1),
+            )
+        result = tail.tile([P, L], F32, name="result")
+        nc.scalar.copy(out=result[:], in_=out_bank[:])
+        nc.sync.dma_start(out=out, in_=result[:])

@@ -64,15 +64,14 @@ def tile_aftblock_pa_t_kernel(tc, z_current, z_window, Wq, Wk, Wv, Wo, out):
         prod_pool = ctx.enter_context(tc.tile_pool(name="prod_pool", bufs=3))
         tail = ctx.enter_context(tc.tile_pool(name="tail", bufs=1))
         sum_banks = ctx.enter_context(tc.psum_pool(name="sum_banks", bufs=1))
-        key_banks = ctx.enter_context(tc.psum_pool(name="key_banks", bufs=4))
+        key_banks = ctx.enter_context(tc.psum_pool(name="key_banks", bufs=2))
+        value_banks = ctx.enter_context(tc.psum_pool(name="value_banks", bufs=2))
         work_banks = ctx.enter_context(tc.psum_pool(name="work_banks", bufs=2))
 
         ident = const.tile([P, P], F32, name="ident")
         make_identity(nc, ident[:])
         den = const.tile([P, A], F32, name="den")
         nc.vector.memset(den[:], EPS)
-
-        ctx.enter_context(tc.manual_schedule())
 
         wk_raw = raw.tile([P, 4, 2 * L], BF16, name="wk_raw")
         wv_raw = raw.tile([P, 4, 2 * L], BF16, name="wv_raw")
@@ -172,12 +171,29 @@ def tile_aftblock_pa_t_kernel(tc, z_current, z_window, Wq, Wk, Wv, Wo, out):
                 made.append(bank)
             return made
 
-        def row_maxima(w):
-            half_max = small.tile([P, HALVES], F32, tag="half_max")
-            for h in range(HALVES):
-                nc.vector.reduce_max(out=half_max[:, h : h + 1], in_=k_banks[w][h][:], axis=AXIS.X)
+        def park_keys(w):
+            e = e_pool.tile([P, A], F32, tag="e")
+            half_max = small.tile([P, 1], F32, tag="half_max")
             row_max = small.tile([P, 1], F32, tag="row_max")
-            nc.vector.reduce_max(out=row_max[:], in_=half_max[:], axis=AXIS.X)
+            nc.vector.tensor_scalar(
+                out=e[:, 0:BANK],
+                in0=k_banks[w][0][:],
+                scalar1=1.0,
+                scalar2=None,
+                op0=ALU.mult,
+                op1=ALU.max,
+                accum_out=half_max[:],
+            )
+            nc.vector.tensor_scalar(
+                out=e[:, BANK:A],
+                in0=k_banks[w][1][:],
+                scalar1=1.0,
+                scalar2=half_max[:, 0:1],
+                op0=ALU.mult,
+                op1=ALU.max,
+                accum_out=row_max[:],
+            )
+            e_tiles[w] = e
             row_maxes[w] = row_max
 
         def spread_maxima(w):
@@ -197,17 +213,11 @@ def tile_aftblock_pa_t_kernel(tc, z_current, z_window, Wq, Wk, Wv, Wo, out):
             neg_maxes[w] = neg_max
 
         def exponentials(w):
-            e = e_pool.tile([P, A], F32, tag="e")
-            for h in range(HALVES):
-                nc.scalar.activation(
-                    out=e[:, h * BANK : (h + 1) * BANK],
-                    in_=k_banks[w][h][:],
-                    func=ACT.Exp,
-                    bias=neg_maxes[w][:, 0:1],
-                    scale=1.0,
-                )
+            e = e_tiles[w]
+            nc.scalar.activation(
+                out=e[:], in_=e[:], func=ACT.Exp, bias=neg_maxes[w][:, 0:1], scale=1.0
+            )
             nc.gpsimd.tensor_tensor(out=den[:], in0=den[:], in1=e[:], op=ALU.add)
-            e_tiles[w] = e
 
         def products(w):
             prod = prod_pool.tile([P, A], F32, tag="prod")
@@ -268,28 +278,28 @@ def tile_aftblock_pa_t_kernel(tc, z_current, z_window, Wq, Wk, Wv, Wo, out):
                     out=scale_t[:, cols], in0=rec_t[:, cols], in1=gate_t[:, cols], op=ALU.mult
                 )
 
-        k_banks[0] = step_matmul(key_banks, "keys", 0, wk_codes, wk_scales)
-        for i in range(STEPS + LAG + 1):
-            j = i - LAG
-            if 0 <= j < STEPS:
-                v_banks[j] = step_matmul(work_banks, "work", j, wv_codes, wv_scales)
-            if i + 1 < STEPS:
-                k_banks[i + 1] = step_matmul(key_banks, "keys", i + 1, wk_codes, wk_scales)
-            if i == STEPS:
+        for n in range(STEPS + LAG + 1):
+            j = n - LAG
+            if n < STEPS:
+                k_banks[n] = step_matmul(key_banks, "keys", n, wk_codes, wk_scales)
+            if n == STEPS + 1:
                 gate()
-            if i < STEPS:
-                row_maxima(i)
+            if 0 <= j < STEPS:
+                v_banks[j] = step_matmul(value_banks, "values", j, wv_codes, wv_scales)
+            if n < STEPS:
+                park_keys(n)
             if 0 <= j - 1:
                 sum_products(j - 1)
+            if 0 <= n - 1 < STEPS:
+                spread_maxima(n - 1)
+            if n == STEPS + 2:
+                gate_over_denominator()
             if 0 <= j < STEPS:
                 products(j)
-            if i < STEPS:
-                spread_maxima(i)
-                step_maximum(i)
-                exponentials(i)
-            if i == STEPS + 1:
-                gate_over_denominator()
-            for job in jobs[i * JOBS_PER_STEP : (i + 1) * JOBS_PER_STEP]:
+            if 0 <= n - 1 < STEPS:
+                step_maximum(n - 1)
+                exponentials(n - 1)
+            for job in jobs[n * JOBS_PER_STEP : (n + 1) * JOBS_PER_STEP]:
                 prepare(job)
 
         h_grouped = tail.tile([P, HALVES * B * PACK], BF16, name="h_grouped", align_bytes=64)

@@ -20,17 +20,15 @@ BANK = 512
 HALVES = A // BANK
 CHUNKS = A // P
 GROUP = 4
-LAG = 8
-JOBS_PER_STEP = 2
+LAG = 6
 
 FLOPS = 2 * B * L * A + 2 * 2 * STEPS * B * L * A + 2 * B * A * L
 
 
-def transpose_and_quantise(nc, banks, stage, ident, row_tiles, codes, scales):
-    count = len(row_tiles)
+def turn_rows(nc, banks, stage, ident, row_tiles):
     grouped = stage.tile([P, GROUP * P * PACK], BF16, tag="grouped", align_bytes=64)
     grouped_words = grouped[:].bitcast(F32)
-    for first in range(0, count, 2):
+    for first in range(0, len(row_tiles), 2):
         pair = row_tiles[first : first + 2]
         width = len(pair) * 2 * P
         turned = banks.tile([P, BANK], F32, tag="work")
@@ -47,8 +45,13 @@ def transpose_and_quantise(nc, banks, stage, ident, row_tiles, codes, scales):
             ),
             in_=turned[:, 0:width].rearrange("p (r u c) -> p r c u", u=2, c=P),
         )
+    return grouped
+
+
+def quantise(nc, grouped, job):
+    row_tiles, codes, scales = job
     nc.vector.quantize_mx(
-        out=codes.bitcast(FP8X4), scales=scales, in_=grouped[:, 0 : count * P * PACK]
+        out=codes.bitcast(FP8X4), scales=scales, in_=grouped[:, 0 : len(row_tiles) * P * PACK]
     )
 
 
@@ -60,7 +63,7 @@ def tile_aftblock_pa_t_kernel(tc, z_current, z_window, Wq, Wk, Wv, Wo, out):
         stage = ctx.enter_context(tc.tile_pool(name="stage", bufs=3))
         quant = ctx.enter_context(tc.tile_pool(name="quant", bufs=1))
         small = ctx.enter_context(tc.tile_pool(name="small", bufs=4))
-        e_pool = ctx.enter_context(tc.tile_pool(name="e_pool", bufs=LAG + 2))
+        e_pool = ctx.enter_context(tc.tile_pool(name="e_pool", bufs=LAG + 3))
         prod_pool = ctx.enter_context(tc.tile_pool(name="prod_pool", bufs=3))
         tail = ctx.enter_context(tc.tile_pool(name="tail", bufs=1))
         sum_banks = ctx.enter_context(tc.psum_pool(name="sum_banks", bufs=1))
@@ -73,6 +76,8 @@ def tile_aftblock_pa_t_kernel(tc, z_current, z_window, Wq, Wk, Wv, Wo, out):
         den = const.tile([P, A], F32, name="den")
         nc.vector.memset(den[:], EPS)
 
+        ctx.enter_context(tc.manual_schedule())
+
         wk_raw = raw.tile([P, 4, 2 * L], BF16, name="wk_raw")
         wv_raw = raw.tile([P, 4, 2 * L], BF16, name="wv_raw")
         wq_raw = raw.tile([P, 4, 2 * L], BF16, name="wq_raw")
@@ -80,9 +85,10 @@ def tile_aftblock_pa_t_kernel(tc, z_current, z_window, Wq, Wk, Wv, Wo, out):
         zc_raw = raw.tile([P, L], BF16, name="zc_raw")
         z_raw = [raw.tile([P, GROUP, L], BF16, name="z_raw%d" % n) for n in range(STEPS // GROUP)]
 
-        def load_weight(tile_ap, weight):
+        def load_weight(tile_ap, weight, g):
             nc.sync.dma_start(
-                out=tile_ap[:], in_=weight.rearrange("(m j e) l -> j m (e l)", m=4, e=2)
+                out=tile_ap[:, 2 * g : 2 * g + 2, :],
+                in_=weight.rearrange("(m j e) l -> j m (e l)", m=4, e=2)[:, 2 * g : 2 * g + 2, :],
             )
 
         def load_steps(n):
@@ -91,14 +97,16 @@ def tile_aftblock_pa_t_kernel(tc, z_current, z_window, Wq, Wk, Wv, Wo, out):
                 in_=z_window[n * GROUP : (n + 1) * GROUP].rearrange("w b l -> b w l"),
             )
 
-        load_weight(wk_raw, Wk)
+        load_weight(wk_raw, Wk, 0)
         load_steps(0)
+        load_weight(wk_raw, Wk, 1)
         load_steps(1)
-        load_steps(2)
-        load_weight(wv_raw, Wv)
-        for n in range(3, STEPS // GROUP):
+        load_weight(wv_raw, Wv, 0)
+        load_weight(wv_raw, Wv, 1)
+        for n in range(2, STEPS // GROUP):
             load_steps(n)
-        load_weight(wq_raw, Wq)
+        load_weight(wq_raw, Wq, 0)
+        load_weight(wq_raw, Wq, 1)
         nc.sync.dma_start(out=zc_raw[:], in_=z_current)
         nc.sync.dma_start(out=wo_raw[:], in_=Wo.rearrange("(c p) a -> p c a", p=P))
 
@@ -136,22 +144,23 @@ def tile_aftblock_pa_t_kernel(tc, z_current, z_window, Wq, Wk, Wv, Wo, out):
             cols = slice(g * L, (g + 1) * L)
             return (rows, wo_codes[:, cols], wo_scales[:, cols])
 
-        def prepare(job):
-            transpose_and_quantise(nc, work_banks, stage, ident, job[0], job[1], job[2])
-
-        prepare(weight_job(wk_raw, wk_codes, wk_scales, 0))
-        prepare(steps_job(0))
-        prepare(weight_job(wk_raw, wk_codes, wk_scales, 1))
-        jobs = [steps_job(1), steps_job(2)]
+        first_jobs = [
+            weight_job(wk_raw, wk_codes, wk_scales, 0),
+            steps_job(0),
+            weight_job(wk_raw, wk_codes, wk_scales, 1),
+        ]
+        for job in first_jobs:
+            quantise(nc, turn_rows(nc, work_banks, stage, ident, job[0]), job)
+        jobs = [steps_job(1)]
         jobs.extend([weight_job(wv_raw, wv_codes, wv_scales, g) for g in range(2)])
-        jobs.extend([steps_job(n) for n in range(3, STEPS // GROUP)])
+        jobs.extend([steps_job(n) for n in range(2, STEPS // GROUP)])
         jobs.extend([weight_job(wq_raw, wq_codes, wq_scales, g) for g in range(2)])
         jobs.append(([zc_raw[:].bitcast(F32)], zc_codes[:], zc_scales[:]))
         jobs.extend([output_weight_job(g) for g in range(2)])
 
         num_t = [sum_banks.tile([P, BANK], F32, name="num_t%d" % g) for g in range(HALVES)]
 
-        k_banks, v_banks, row_maxes, spreads, neg_maxes, e_tiles, prod_tiles = {}, {}, {}, {}, {}, {}, {}
+        k_banks, v_banks, maxima, spreads, neg_maxes, e_tiles, prod_tiles = {}, {}, {}, {}, {}, {}, {}
 
         def step_matmul(banks, tag, w, codes, scales):
             step = slice(w * B, (w + 1) * B)
@@ -171,36 +180,25 @@ def tile_aftblock_pa_t_kernel(tc, z_current, z_window, Wq, Wk, Wv, Wo, out):
                 made.append(bank)
             return made
 
-        def park_keys(w):
-            e = e_pool.tile([P, A], F32, tag="e")
-            half_max = small.tile([P, 1], F32, tag="half_max")
-            row_max = small.tile([P, 1], F32, tag="row_max")
+        def park_keys(w, h):
+            if h == 0:
+                e_tiles[w] = e_pool.tile([P, A], F32, tag="e", name="e")
+                maxima[w] = small.tile([P, HALVES], F32, tag="maxima", name="maxima")
             nc.vector.tensor_scalar(
-                out=e[:, 0:BANK],
-                in0=k_banks[w][0][:],
+                out=e_tiles[w][:, h * BANK : (h + 1) * BANK],
+                in0=k_banks[w][h][:],
                 scalar1=1.0,
-                scalar2=None,
+                scalar2=(None if h == 0 else maxima[w][:, h - 1 : h]),
                 op0=ALU.mult,
                 op1=ALU.max,
-                accum_out=half_max[:],
+                accum_out=maxima[w][:, h : h + 1],
             )
-            nc.vector.tensor_scalar(
-                out=e[:, BANK:A],
-                in0=k_banks[w][1][:],
-                scalar1=1.0,
-                scalar2=half_max[:, 0:1],
-                op0=ALU.mult,
-                op1=ALU.max,
-                accum_out=row_max[:],
-            )
-            e_tiles[w] = e
-            row_maxes[w] = row_max
 
         def spread_maxima(w):
             spread = work_banks.tile([P, BANK], F32, tag="work")
             nc.tensor.transpose(
                 out=spread[:, 0:P],
-                in_=row_maxes[w][:, 0:1].to_broadcast([P, P]),
+                in_=maxima[w][:, HALVES - 1 : HALVES].to_broadcast([P, P]),
                 identity=ident[:],
             )
             spreads[w] = spread
@@ -262,24 +260,32 @@ def tile_aftblock_pa_t_kernel(tc, z_current, z_window, Wq, Wk, Wv, Wo, out):
                     out=gate_t[:, g * BANK : (g + 1) * BANK], in_=q_t[:], func=ACT.Sigmoid
                 )
 
-        def gate_over_denominator():
+        den_t = {}
+
+        def turn_denominator():
             for g in range(HALVES):
-                cols = slice(g * BANK, (g + 1) * BANK)
-                den_t = key_banks.tile([P, BANK], F32, tag="keys", name="den_t")
+                den_t[g] = key_banks.tile([P, BANK], F32, tag="keys", name="den_t")
                 for t in range(PACK):
                     c = g * PACK + t
                     nc.tensor.transpose(
-                        out=den_t[:, t * B : (t + 1) * B],
+                        out=den_t[g][:, t * B : (t + 1) * B],
                         in_=den[:, c * P : (c + 1) * P],
                         identity=ident[:],
                     )
-                nc.vector.reciprocal(out=rec_t[:, cols], in_=den_t[:])
-                nc.gpsimd.tensor_tensor(
+
+        def gate_over_denominator():
+            for g in range(HALVES):
+                cols = slice(g * BANK, (g + 1) * BANK)
+                nc.vector.reciprocal(out=rec_t[:, cols], in_=den_t[g][:])
+                nc.vector.tensor_tensor(
                     out=scale_t[:, cols], in0=rec_t[:, cols], in1=gate_t[:, cols], op=ALU.mult
                 )
 
+        turned = {}
         for n in range(STEPS + LAG + 1):
             j = n - LAG
+            if 1 <= n <= STEPS:
+                exponentials(n - 1)
             if n < STEPS:
                 k_banks[n] = step_matmul(key_banks, "keys", n, wk_codes, wk_scales)
             if n == STEPS + 1:
@@ -287,20 +293,25 @@ def tile_aftblock_pa_t_kernel(tc, z_current, z_window, Wq, Wk, Wv, Wo, out):
             if 0 <= j < STEPS:
                 v_banks[j] = step_matmul(value_banks, "values", j, wv_codes, wv_scales)
             if n < STEPS:
-                park_keys(n)
-            if 0 <= j - 1:
+                park_keys(n, 0)
+            if 1 <= n <= len(jobs):
+                quantise(nc, turned[n - 1], jobs[n - 1])
+            if n < STEPS:
+                park_keys(n, 1)
+            if 1 <= j:
                 sum_products(j - 1)
-            if 0 <= n - 1 < STEPS:
-                spread_maxima(n - 1)
-            if n == STEPS + 2:
-                gate_over_denominator()
+            if n < len(jobs):
+                turned[n] = turn_rows(nc, work_banks, stage, ident, jobs[n][0])
+            if n < STEPS:
+                spread_maxima(n)
+            if n == STEPS + 3:
+                turn_denominator()
             if 0 <= j < STEPS:
                 products(j)
-            if 0 <= n - 1 < STEPS:
-                step_maximum(n - 1)
-                exponentials(n - 1)
-            for job in jobs[n * JOBS_PER_STEP : (n + 1) * JOBS_PER_STEP]:
-                prepare(job)
+            if n < STEPS:
+                step_maximum(n)
+            if n == STEPS + 3:
+                gate_over_denominator()
 
         h_grouped = tail.tile([P, HALVES * B * PACK], BF16, name="h_grouped", align_bytes=64)
         h_codes = tail.tile([P, HALVES * B], U32, name="h_codes", align_bytes=64)

@@ -180,25 +180,22 @@ def tile_aftblock_pa_t_kernel(tc, z_current, z_window, Wq, Wk, Wv, Wo, out):
                 made.append(bank)
             return made
 
-        def park_keys(w, h):
-            if h == 0:
-                e_tiles[w] = e_pool.tile([P, A], F32, tag="e", name="e")
-                maxima[w] = small.tile([P, HALVES], F32, tag="maxima", name="maxima")
-            nc.vector.tensor_scalar(
-                out=e_tiles[w][:, h * BANK : (h + 1) * BANK],
-                in0=k_banks[w][h][:],
-                scalar1=1.0,
-                scalar2=(None if h == 0 else maxima[w][:, h - 1 : h]),
-                op0=ALU.mult,
-                op1=ALU.max,
-                accum_out=maxima[w][:, h : h + 1],
-            )
+        def park_keys(w):
+            e = e_pool.tile([P, A], F32, tag="e")
+            for h in range(HALVES):
+                nc.scalar.copy(out=e[:, h * BANK : (h + 1) * BANK], in_=k_banks[w][h][:])
+            e_tiles[w] = e
+
+        def row_maxima(w):
+            row_max = small.tile([P, 1], F32, tag="row_max")
+            nc.vector.reduce_max(out=row_max[:], in_=e_tiles[w][:], axis=AXIS.X)
+            maxima[w] = row_max
 
         def spread_maxima(w):
             spread = work_banks.tile([P, BANK], F32, tag="work")
             nc.tensor.transpose(
                 out=spread[:, 0:P],
-                in_=maxima[w][:, HALVES - 1 : HALVES].to_broadcast([P, P]),
+                in_=maxima[w][:, 0:1].to_broadcast([P, P]),
                 identity=ident[:],
             )
             spreads[w] = spread
@@ -284,33 +281,33 @@ def tile_aftblock_pa_t_kernel(tc, z_current, z_window, Wq, Wk, Wv, Wo, out):
         turned = {}
         for n in range(STEPS + LAG + 1):
             j = n - LAG
-            if 1 <= n <= STEPS:
-                exponentials(n - 1)
+            if 2 <= n <= STEPS + 1:
+                exponentials(n - 2)
             if n < STEPS:
                 k_banks[n] = step_matmul(key_banks, "keys", n, wk_codes, wk_scales)
-            if n == STEPS + 1:
+            if n == STEPS + 2:
                 gate()
             if 0 <= j < STEPS:
                 v_banks[j] = step_matmul(value_banks, "values", j, wv_codes, wv_scales)
             if n < STEPS:
-                park_keys(n, 0)
+                park_keys(n)
+            if 1 <= n <= STEPS:
+                row_maxima(n - 1)
             if 1 <= n <= len(jobs):
                 quantise(nc, turned[n - 1], jobs[n - 1])
-            if n < STEPS:
-                park_keys(n, 1)
             if 1 <= j:
                 sum_products(j - 1)
             if n < len(jobs):
                 turned[n] = turn_rows(nc, work_banks, stage, ident, jobs[n][0])
-            if n < STEPS:
-                spread_maxima(n)
-            if n == STEPS + 3:
+            if 1 <= n <= STEPS:
+                spread_maxima(n - 1)
+            if n == STEPS + 4:
                 turn_denominator()
             if 0 <= j < STEPS:
                 products(j)
-            if n < STEPS:
-                step_maximum(n)
-            if n == STEPS + 3:
+            if 1 <= n <= STEPS:
+                step_maximum(n - 1)
+            if n == STEPS + 4:
                 gate_over_denominator()
 
         h_grouped = tail.tile([P, HALVES * B * PACK], BF16, name="h_grouped", align_bytes=64)

@@ -20,38 +20,23 @@ BANK = 512
 HALVES = A // BANK
 CHUNKS = A // P
 GROUP = 4
-LAG = 6
+LAG = 3
 
 FLOPS = 2 * B * L * A + 2 * 2 * STEPS * B * L * A + 2 * B * A * L
 
 
-def turn_rows(nc, banks, stage, ident, row_tiles):
-    grouped = stage.tile([P, GROUP * P * PACK], BF16, tag="grouped", align_bytes=64)
-    grouped_words = grouped[:].bitcast(F32)
-    for first in range(0, len(row_tiles), 2):
-        pair = row_tiles[first : first + 2]
-        width = len(pair) * 2 * P
-        turned = banks.tile([P, BANK], F32, tag="work")
-        for r, words in enumerate(pair):
-            for u in range(2):
-                nc.tensor.transpose(
-                    out=turned[:, (2 * r + u) * P : (2 * r + u + 1) * P],
-                    in_=words[:, u * P : (u + 1) * P],
-                    identity=ident[:],
-                )
-        nc.scalar.copy(
-            out=grouped_words[:, first * 2 * P : first * 2 * P + width].rearrange(
-                "p (r c u) -> p r c u", c=P, u=2
-            ),
-            in_=turned[:, 0:width].rearrange("p (r u c) -> p r c u", u=2, c=P),
-        )
-    return grouped
-
-
-def quantise(nc, grouped, job):
-    row_tiles, codes, scales = job
-    nc.vector.quantize_mx(
-        out=codes.bitcast(FP8X4), scales=scales, in_=grouped[:, 0 : len(row_tiles) * P * PACK]
+def turn_pair(nc, bank, ident, pair, grouped_words):
+    for r, words in enumerate(pair):
+        for u in range(2):
+            nc.tensor.transpose(
+                out=bank[:, (2 * r + u) * P : (2 * r + u + 1) * P],
+                in_=words[:, u * P : (u + 1) * P],
+                identity=ident[:],
+            )
+    width = len(pair) * 2 * P
+    nc.scalar.copy(
+        out=grouped_words[:, 0:width].rearrange("p (r c u) -> p r c u", c=P, u=2),
+        in_=bank[:, 0:width].rearrange("p (r u c) -> p r c u", u=2, c=P),
     )
 
 
@@ -60,16 +45,16 @@ def tile_aftblock_pa_t_kernel(tc, z_current, z_window, Wq, Wk, Wv, Wo, out):
     with ExitStack() as ctx:
         const = ctx.enter_context(tc.tile_pool(name="const", bufs=1))
         raw = ctx.enter_context(tc.tile_pool(name="raw", bufs=1))
-        stage = ctx.enter_context(tc.tile_pool(name="stage", bufs=3))
+        stage = ctx.enter_context(tc.tile_pool(name="stage", bufs=4))
         quant = ctx.enter_context(tc.tile_pool(name="quant", bufs=1))
         small = ctx.enter_context(tc.tile_pool(name="small", bufs=4))
-        e_pool = ctx.enter_context(tc.tile_pool(name="e_pool", bufs=LAG + 3))
+        e_pool = ctx.enter_context(tc.tile_pool(name="e_pool", bufs=LAG + 4))
         prod_pool = ctx.enter_context(tc.tile_pool(name="prod_pool", bufs=3))
         tail = ctx.enter_context(tc.tile_pool(name="tail", bufs=1))
         sum_banks = ctx.enter_context(tc.psum_pool(name="sum_banks", bufs=1))
         key_banks = ctx.enter_context(tc.psum_pool(name="key_banks", bufs=2))
         value_banks = ctx.enter_context(tc.psum_pool(name="value_banks", bufs=2))
-        work_banks = ctx.enter_context(tc.psum_pool(name="work_banks", bufs=2))
+        single_banks = ctx.enter_context(tc.psum_pool(name="single_banks", bufs=1))
 
         ident = const.tile([P, P], F32, name="ident")
         make_identity(nc, ident[:])
@@ -100,8 +85,8 @@ def tile_aftblock_pa_t_kernel(tc, z_current, z_window, Wq, Wk, Wv, Wo, out):
         load_weight(wk_raw, Wk, 0)
         load_steps(0)
         load_weight(wk_raw, Wk, 1)
-        load_steps(1)
         load_weight(wv_raw, Wv, 0)
+        load_steps(1)
         load_weight(wv_raw, Wv, 1)
         for n in range(2, STEPS // GROUP):
             load_steps(n)
@@ -123,7 +108,7 @@ def tile_aftblock_pa_t_kernel(tc, z_current, z_window, Wq, Wk, Wv, Wo, out):
         wo_codes = quant.tile([P, 2 * L], U32, name="wo_codes", align_bytes=64)
         wo_scales = quant.tile([P, 2 * L], U8, name="wo_scales", align_bytes=64)
 
-        def weight_job(raw_tile, codes, scales, g):
+        def weight_group(raw_tile, codes, scales, g):
             words = raw_tile[:].bitcast(F32)
             rows = [
                 words[:, 2 * g + u, e * (L // 2) : (e + 1) * (L // 2)]
@@ -133,30 +118,54 @@ def tile_aftblock_pa_t_kernel(tc, z_current, z_window, Wq, Wk, Wv, Wo, out):
             cols = slice(g * BANK, (g + 1) * BANK)
             return (rows, codes[:, cols], scales[:, cols])
 
-        def steps_job(n):
+        def steps_group(n):
             words = z_raw[n][:].bitcast(F32)
             cols = slice(n * GROUP * B, (n + 1) * GROUP * B)
             return ([words[:, s, :] for s in range(GROUP)], z_codes[:, cols], z_scales[:, cols])
 
-        def output_weight_job(g):
+        def output_weight_group(g):
             words = wo_raw[:].bitcast(F32)
             rows = [words[:, c, g * (BANK // 2) : (g + 1) * (BANK // 2)] for c in range(L // P)]
             cols = slice(g * L, (g + 1) * L)
             return (rows, wo_codes[:, cols], wo_scales[:, cols])
 
-        first_jobs = [
-            weight_job(wk_raw, wk_codes, wk_scales, 0),
-            steps_job(0),
-            weight_job(wk_raw, wk_codes, wk_scales, 1),
-        ]
-        for job in first_jobs:
-            quantise(nc, turn_rows(nc, work_banks, stage, ident, job[0]), job)
-        jobs = [steps_job(1)]
-        jobs.extend([weight_job(wv_raw, wv_codes, wv_scales, g) for g in range(2)])
-        jobs.extend([steps_job(n) for n in range(2, STEPS // GROUP)])
-        jobs.extend([weight_job(wq_raw, wq_codes, wq_scales, g) for g in range(2)])
-        jobs.append(([zc_raw[:].bitcast(F32)], zc_codes[:], zc_scales[:]))
-        jobs.extend([output_weight_job(g) for g in range(2)])
+        def new_grouped():
+            grouped = stage.tile([P, GROUP * P * PACK], BF16, tag="grouped", align_bytes=64)
+            return grouped
+
+        def turn_half(group, grouped, half, banks, tag):
+            bank = banks.tile([P, BANK], F32, tag=tag, name="turned")
+            words = grouped[:].bitcast(F32)[:, half * BANK : (half + 1) * BANK]
+            turn_pair(nc, bank, ident, group[0][2 * half : 2 * half + 2], words)
+
+        def quantise(group, grouped):
+            nc.vector.quantize_mx(
+                out=group[1].bitcast(FP8X4),
+                scales=group[2],
+                in_=grouped[:, 0 : len(group[0]) * P * PACK],
+            )
+
+        def turn_whole(group):
+            grouped = new_grouped()
+            for half in range(2):
+                turn_half(group, grouped, half, value_banks, "values")
+            return grouped
+
+        for group in [
+            weight_group(wk_raw, wk_codes, wk_scales, 0),
+            steps_group(0),
+            weight_group(wk_raw, wk_codes, wk_scales, 1),
+        ]:
+            quantise(group, turn_whole(group))
+        value_groups = [weight_group(wv_raw, wv_codes, wv_scales, g) for g in range(2)]
+        later_groups = [steps_group(n) for n in range(1, STEPS // GROUP)]
+        later_groups.extend([weight_group(wq_raw, wq_codes, wq_scales, g) for g in range(2)])
+        later_groups.append(([zc_raw[:].bitcast(F32)], zc_codes[:], zc_scales[:]))
+        later_groups.extend([output_weight_group(g) for g in range(2)])
+        stream = []
+        for index, group in enumerate(later_groups):
+            halves = (len(group[0]) + 1) // 2
+            stream.extend([(index, half, half == halves - 1) for half in range(halves)])
 
         num_t = [sum_banks.tile([P, BANK], F32, name="num_t%d" % g) for g in range(HALVES)]
 
@@ -180,22 +189,25 @@ def tile_aftblock_pa_t_kernel(tc, z_current, z_window, Wq, Wk, Wv, Wo, out):
                 made.append(bank)
             return made
 
-        def park_keys(w):
-            e = e_pool.tile([P, A], F32, tag="e")
-            for h in range(HALVES):
-                nc.scalar.copy(out=e[:, h * BANK : (h + 1) * BANK], in_=k_banks[w][h][:])
-            e_tiles[w] = e
-
-        def row_maxima(w):
-            row_max = small.tile([P, 1], F32, tag="row_max")
-            nc.vector.reduce_max(out=row_max[:], in_=e_tiles[w][:], axis=AXIS.X)
-            maxima[w] = row_max
+        def park_keys(w, h):
+            if h == 0:
+                e_tiles[w] = e_pool.tile([P, A], F32, tag="e", name="e")
+                maxima[w] = small.tile([P, HALVES], F32, tag="maxima", name="maxima")
+            nc.vector.tensor_scalar(
+                out=e_tiles[w][:, h * BANK : (h + 1) * BANK],
+                in0=k_banks[w][h][:],
+                scalar1=1.0,
+                scalar2=(None if h == 0 else maxima[w][:, h - 1 : h]),
+                op0=ALU.mult,
+                op1=ALU.max,
+                accum_out=maxima[w][:, h : h + 1],
+            )
 
         def spread_maxima(w):
-            spread = work_banks.tile([P, BANK], F32, tag="work")
+            spread = single_banks.tile([P, BANK], F32, tag="spread")
             nc.tensor.transpose(
                 out=spread[:, 0:P],
-                in_=maxima[w][:, 0:1].to_broadcast([P, P]),
+                in_=maxima[w][:, HALVES - 1 : HALVES].to_broadcast([P, P]),
                 identity=ident[:],
             )
             spreads[w] = spread
@@ -212,7 +224,8 @@ def tile_aftblock_pa_t_kernel(tc, z_current, z_window, Wq, Wk, Wv, Wo, out):
             nc.scalar.activation(
                 out=e[:], in_=e[:], func=ACT.Exp, bias=neg_maxes[w][:, 0:1], scale=1.0
             )
-            nc.gpsimd.tensor_tensor(out=den[:], in0=den[:], in1=e[:], op=ALU.add)
+            if w < STEPS - 1:
+                nc.gpsimd.tensor_tensor(out=den[:], in0=den[:], in1=e[:], op=ALU.add)
 
         def products(w):
             prod = prod_pool.tile([P, A], F32, tag="prod")
@@ -223,17 +236,21 @@ def tile_aftblock_pa_t_kernel(tc, z_current, z_window, Wq, Wk, Wv, Wo, out):
                 )
             prod_tiles[w] = prod
 
-        def sum_products(w):
-            for c in range(CHUNKS):
-                g, t = c // PACK, c % PACK
+        def add_transposed(bank, source, g, first, last):
+            for t in range(PACK):
+                c = g * PACK + t
                 nc.tensor.matmul(
-                    out=num_t[g][:, t * B : (t + 1) * B],
-                    lhsT=prod_tiles[w][:, c * P : (c + 1) * P],
+                    out=bank[:, t * B : (t + 1) * B],
+                    lhsT=source[:, c * P : (c + 1) * P],
                     rhs=ident[:],
                     is_transpose=True,
-                    start=(w == 0 and t == 0),
-                    stop=(w == STEPS - 1 and t == PACK - 1),
+                    start=(first and t == 0),
+                    stop=(last and t == PACK - 1),
                 )
+
+        def sum_products(w):
+            for g in range(HALVES):
+                add_transposed(num_t[g], prod_tiles[w], g, w == 0, w == STEPS - 1)
 
         gate_t = tail.tile([P, A], F32, name="gate_t")
         rec_t = tail.tile([P, A], F32, name="rec_t")
@@ -241,7 +258,7 @@ def tile_aftblock_pa_t_kernel(tc, z_current, z_window, Wq, Wk, Wv, Wo, out):
 
         def gate():
             for g in range(HALVES):
-                q_t = key_banks.tile([P, BANK], F32, tag="keys", name="q_t")
+                q_t = single_banks.tile([P, BANK], F32, tag=("turn", "spread")[g], name="q_t")
                 for t in range(PACK):
                     c = g * PACK + t
                     nc.tensor.matmul_mx(
@@ -262,13 +279,8 @@ def tile_aftblock_pa_t_kernel(tc, z_current, z_window, Wq, Wk, Wv, Wo, out):
         def turn_denominator():
             for g in range(HALVES):
                 den_t[g] = key_banks.tile([P, BANK], F32, tag="keys", name="den_t")
-                for t in range(PACK):
-                    c = g * PACK + t
-                    nc.tensor.transpose(
-                        out=den_t[g][:, t * B : (t + 1) * B],
-                        in_=den[:, c * P : (c + 1) * P],
-                        identity=ident[:],
-                    )
+                add_transposed(den_t[g], den, g, True, False)
+                add_transposed(den_t[g], e_tiles[STEPS - 1], g, False, True)
 
         def gate_over_denominator():
             for g in range(HALVES):
@@ -278,36 +290,43 @@ def tile_aftblock_pa_t_kernel(tc, z_current, z_window, Wq, Wk, Wv, Wo, out):
                     out=scale_t[:, cols], in0=rec_t[:, cols], in1=gate_t[:, cols], op=ALU.mult
                 )
 
-        turned = {}
+        value_grouped, later_grouped = {}, {}
         for n in range(STEPS + LAG + 1):
             j = n - LAG
-            if 2 <= n <= STEPS + 1:
+            if 2 <= n < STEPS + 2:
                 exponentials(n - 2)
             if n < STEPS:
                 k_banks[n] = step_matmul(key_banks, "keys", n, wk_codes, wk_scales)
-            if n == STEPS + 2:
+            if n == STEPS + 1:
                 gate()
             if 0 <= j < STEPS:
                 v_banks[j] = step_matmul(value_banks, "values", j, wv_codes, wv_scales)
             if n < STEPS:
-                park_keys(n)
-            if 1 <= n <= STEPS:
-                row_maxima(n - 1)
-            if 1 <= n <= len(jobs):
-                quantise(nc, turned[n - 1], jobs[n - 1])
-            if 1 <= j:
-                sum_products(j - 1)
-            if n < len(jobs):
-                turned[n] = turn_rows(nc, work_banks, stage, ident, jobs[n][0])
-            if 1 <= n <= STEPS:
+                park_keys(n, 0)
+            if 1 <= n <= len(value_groups):
+                quantise(value_groups[n - 1], value_grouped[n - 1])
+            if 1 <= n <= len(stream) and stream[n - 1][2]:
+                quantise(later_groups[stream[n - 1][0]], later_grouped[stream[n - 1][0]])
+            if n < STEPS:
+                park_keys(n, 1)
+            if 1 <= n < STEPS + 1:
                 spread_maxima(n - 1)
-            if n == STEPS + 4:
+            if n == STEPS + 2:
                 turn_denominator()
+            if n < len(value_groups):
+                value_grouped[n] = turn_whole(value_groups[n])
+            if n < len(stream):
+                index, half = stream[n][0], stream[n][1]
+                if half == 0:
+                    later_grouped[index] = new_grouped()
+                turn_half(later_groups[index], later_grouped[index], half, single_banks, "turn")
+            if 1 <= j < STEPS + 1:
+                sum_products(j - 1)
             if 0 <= j < STEPS:
                 products(j)
-            if 1 <= n <= STEPS:
+            if 1 <= n < STEPS + 1:
                 step_maximum(n - 1)
-            if n == STEPS + 4:
+            if n == STEPS + 2:
                 gate_over_denominator()
 
         h_grouped = tail.tile([P, HALVES * B * PACK], BF16, name="h_grouped", align_bytes=64)
@@ -322,7 +341,7 @@ def tile_aftblock_pa_t_kernel(tc, z_current, z_window, Wq, Wk, Wv, Wo, out):
                 op=ALU.mult,
             )
         nc.vector.quantize_mx(out=h_codes[:].bitcast(FP8X4), scales=h_scales[:], in_=h_grouped[:])
-        out_bank = work_banks.tile([P, BANK], F32, tag="work")
+        out_bank = single_banks.tile([P, BANK], F32, tag="turn")
         for g in range(HALVES):
             nc.tensor.matmul_mx(
                 out=out_bank[:],

from contextlib import ExitStack

import concourse.mybir as mybir
from concourse.masks import make_identity

F32 = mybir.dt.float32
BF16 = mybir.dt.bfloat16
U32 = mybir.dt.uint32
U8 = mybir.dt.uint8
FP8X4 = mybir.dt.float8_e4m3fn_x4
ACT = mybir.ActivationFunctionType
ALU = mybir.AluOpType
AXIS = mybir.AxisListType

P = 128
B, L, A, STEPS = 128, 512, 1024, 32
EPS = 1e-8
PACK = 4
BANK = 512
HALVES = A // BANK
CHUNKS = A // P
GROUP = 4
LAG = 3

FLOPS = 2 * B * L * A + 2 * 2 * STEPS * B * L * A + 2 * B * A * L


def turn_pair(nc, bank, ident, pair, grouped_words):
    for r, words in enumerate(pair):
        for u in range(2):
            nc.tensor.transpose(
                out=bank[:, (2 * r + u) * P : (2 * r + u + 1) * P],
                in_=words[:, u * P : (u + 1) * P],
                identity=ident[:],
            )
    width = len(pair) * 2 * P
    nc.scalar.copy(
        out=grouped_words[:, 0:width].rearrange("p (r c u) -> p r c u", c=P, u=2),
        in_=bank[:, 0:width].rearrange("p (r u c) -> p r c u", u=2, c=P),
    )


def tile_aftblock_pa_t_kernel(tc, z_current, z_window, Wq, Wk, Wv, Wo, out):
    nc = tc.nc
    with ExitStack() as ctx:
        const = ctx.enter_context(tc.tile_pool(name="const", bufs=1))
        raw = ctx.enter_context(tc.tile_pool(name="raw", bufs=1))
        stage = ctx.enter_context(tc.tile_pool(name="stage", bufs=4))
        quant = ctx.enter_context(tc.tile_pool(name="quant", bufs=1))
        small = ctx.enter_context(tc.tile_pool(name="small", bufs=4))
        e_pool = ctx.enter_context(tc.tile_pool(name="e_pool", bufs=LAG + 4))
        prod_pool = ctx.enter_context(tc.tile_pool(name="prod_pool", bufs=3))
        tail = ctx.enter_context(tc.tile_pool(name="tail", bufs=1))
        sum_banks = ctx.enter_context(tc.psum_pool(name="sum_banks", bufs=1))
        key_banks = ctx.enter_context(tc.psum_pool(name="key_banks", bufs=2))
        value_banks = ctx.enter_context(tc.psum_pool(name="value_banks", bufs=2))
        single_banks = ctx.enter_context(tc.psum_pool(name="single_banks", bufs=1))

        ident = const.tile([P, P], F32, name="ident")
        make_identity(nc, ident[:])
        den = const.tile([P, A], F32, name="den")
        nc.vector.memset(den[:], EPS)

        ctx.enter_context(tc.manual_schedule())

        wk_raw = raw.tile([P, 4, 2 * L], BF16, name="wk_raw")
        wv_raw = raw.tile([P, 4, 2 * L], BF16, name="wv_raw")
        wq_raw = raw.tile([P, 4, 2 * L], BF16, name="wq_raw")
        wo_raw = raw.tile([P, L // P, A], BF16, name="wo_raw")
        zc_raw = raw.tile([P, L], BF16, name="zc_raw")
        z_raw = [raw.tile([P, GROUP, L], BF16, name="z_raw%d" % n) for n in range(STEPS // GROUP)]

        def load_weight(tile_ap, weight, g):
            nc.sync.dma_start(
                out=tile_ap[:, 2 * g : 2 * g + 2, :],
                in_=weight.rearrange("(m j e) l -> j m (e l)", m=4, e=2)[:, 2 * g : 2 * g + 2, :],
            )

        def load_steps(n):
            nc.sync.dma_start(
                out=z_raw[n][:],
                in_=z_window[n * GROUP : (n + 1) * GROUP].rearrange("w b l -> b w l"),
            )

        load_weight(wk_raw, Wk, 0)
        load_steps(0)
        load_weight(wk_raw, Wk, 1)
        load_weight(wv_raw, Wv, 0)
        load_steps(1)
        load_weight(wv_raw, Wv, 1)
        for n in range(2, STEPS // GROUP):
            load_steps(n)
        load_weight(wq_raw, Wq, 0)
        load_weight(wq_raw, Wq, 1)
        nc.sync.dma_start(out=zc_raw[:], in_=z_current)
        nc.sync.dma_start(out=wo_raw[:], in_=Wo.rearrange("(c p) a -> p c a", p=P))

        z_codes = quant.tile([P, STEPS * B], U32, name="z_codes", align_bytes=64)
        z_scales = quant.tile([P, STEPS * B], U8, name="z_scales", align_bytes=64)
        zc_codes = quant.tile([P, B], U32, name="zc_codes", align_bytes=64)
        zc_scales = quant.tile([P, B], U8, name="zc_scales", align_bytes=64)
        wk_codes = quant.tile([P, A], U32, name="wk_codes", align_bytes=64)
        wk_scales = quant.tile([P, A], U8, name="wk_scales", align_bytes=64)
        wv_codes = quant.tile([P, A], U32, name="wv_codes", align_bytes=64)
        wv_scales = quant.tile([P, A], U8, name="wv_scales", align_bytes=64)
        wq_codes = quant.tile([P, A], U32, name="wq_codes", align_bytes=64)
        wq_scales = quant.tile([P, A], U8, name="wq_scales", align_bytes=64)
        wo_codes = quant.tile([P, 2 * L], U32, name="wo_codes", align_bytes=64)
        wo_scales = quant.tile([P, 2 * L], U8, name="wo_scales", align_bytes=64)

        def weight_group(raw_tile, codes, scales, g):
            words = raw_tile[:].bitcast(F32)
            rows = [
                words[:, 2 * g + u, e * (L // 2) : (e + 1) * (L // 2)]
                for u in range(2)
                for e in range(2)
            ]
            cols = slice(g * BANK, (g + 1) * BANK)
            return (rows, codes[:, cols], scales[:, cols])

        def steps_group(n):
            words = z_raw[n][:].bitcast(F32)
            cols = slice(n * GROUP * B, (n + 1) * GROUP * B)
            return ([words[:, s, :] for s in range(GROUP)], z_codes[:, cols], z_scales[:, cols])

        def output_weight_group(g):
            words = wo_raw[:].bitcast(F32)
            rows = [words[:, c, g * (BANK // 2) : (g + 1) * (BANK // 2)] for c in range(L // P)]
            cols = slice(g * L, (g + 1) * L)
            return (rows, wo_codes[:, cols], wo_scales[:, cols])

        def new_grouped():
            grouped = stage.tile([P, GROUP * P * PACK], BF16, tag="grouped", align_bytes=64)
            return grouped

        def turn_half(group, grouped, half, banks, tag):
            bank = banks.tile([P, BANK], F32, tag=tag, name="turned")
            words = grouped[:].bitcast(F32)[:, half * BANK : (half + 1) * BANK]
            turn_pair(nc, bank, ident, group[0][2 * half : 2 * half + 2], words)

        def quantise(group, grouped):
            nc.vector.quantize_mx(
                out=group[1].bitcast(FP8X4),
                scales=group[2],
                in_=grouped[:, 0 : len(group[0]) * P * PACK],
            )

        def turn_whole(group):
            grouped = new_grouped()
            for half in range(2):
                turn_half(group, grouped, half, value_banks, "values")
            return grouped

        for group in [
            weight_group(wk_raw, wk_codes, wk_scales, 0),
            steps_group(0),
            weight_group(wk_raw, wk_codes, wk_scales, 1),
        ]:
            quantise(group, turn_whole(group))
        value_groups = [weight_group(wv_raw, wv_codes, wv_scales, g) for g in range(2)]
        later_groups = [steps_group(n) for n in range(1, STEPS // GROUP)]
        later_groups.extend([weight_group(wq_raw, wq_codes, wq_scales, g) for g in range(2)])
        later_groups.append(([zc_raw[:].bitcast(F32)], zc_codes[:], zc_scales[:]))
        later_groups.extend([output_weight_group(g) for g in range(2)])
        stream = []
        for index, group in enumerate(later_groups):
            halves = (len(group[0]) + 1) // 2
            stream.extend([(index, half, half == halves - 1) for half in range(halves)])

        num_t = [sum_banks.tile([P, BANK], F32, name="num_t%d" % g) for g in range(HALVES)]

        k_banks, v_banks, maxima, spreads, neg_maxes, e_tiles, prod_tiles = {}, {}, {}, {}, {}, {}, {}

        def step_matmul(banks, tag, w, codes, scales):
            step = slice(w * B, (w + 1) * B)
            made = []
            for h in range(HALVES):
                cols = slice(h * BANK, (h + 1) * BANK)
                bank = banks.tile([P, BANK], F32, tag=tag, name="bank_" + tag)
                nc.tensor.matmul_mx(
                    out=bank[:],
                    lhsT=z_codes[:, step].bitcast(FP8X4),
                    lhsT_scale=z_scales[:, step],
                    rhs=codes[:, cols].bitcast(FP8X4),
                    rhs_scale=scales[:, cols],
                    start=True,
                    stop=True,
                )
                made.append(bank)
            return made

        def park_keys(w, h):
            if h == 0:
                e_tiles[w] = e_pool.tile([P, A], F32, tag="e", name="e")
                maxima[w] = small.tile([P, HALVES], F32, tag="maxima", name="maxima")
            nc.vector.tensor_scalar(
                out=e_tiles[w][:, h * BANK : (h + 1) * BANK],
                in0=k_banks[w][h][:],
                scalar1=1.0,
                scalar2=(None if h == 0 else maxima[w][:, h - 1 : h]),
                op0=ALU.mult,
                op1=ALU.max,
                accum_out=maxima[w][:, h : h + 1],
            )

        def spread_maxima(w):
            spread = single_banks.tile([P, BANK], F32, tag="spread")
            nc.tensor.transpose(
                out=spread[:, 0:P],
                in_=maxima[w][:, HALVES - 1 : HALVES].to_broadcast([P, P]),
                identity=ident[:],
            )
            spreads[w] = spread

        def step_maximum(w):
            neg_max = small.tile([P, 1], F32, tag="neg_max")
            nc.vector.tensor_reduce(
                out=neg_max[:], in_=spreads[w][:, 0:P], axis=AXIS.X, op=ALU.max, negate=True
            )
            neg_maxes[w] = neg_max

        def exponentials(w):
            e = e_tiles[w]
            nc.scalar.activation(
                out=e[:], in_=e[:], func=ACT.Exp, bias=neg_maxes[w][:, 0:1], scale=1.0
            )
            if w < STEPS - 1:
                nc.gpsimd.tensor_tensor(out=den[:], in0=den[:], in1=e[:], op=ALU.add)

        def products(w):
            prod = prod_pool.tile([P, A], F32, tag="prod")
            for h in range(HALVES):
                cols = slice(h * BANK, (h + 1) * BANK)
                nc.vector.tensor_tensor(
                    out=prod[:, cols], in0=v_banks[w][h][:], in1=e_tiles[w][:, cols], op=ALU.mult
                )
            prod_tiles[w] = prod

        def add_transposed(bank, source, g, first, last):
            for t in range(PACK):
                c = g * PACK + t
                nc.tensor.matmul(
                    out=bank[:, t * B : (t + 1) * B],
                    lhsT=source[:, c * P : (c + 1) * P],
                    rhs=ident[:],
                    is_transpose=True,
                    start=(first and t == 0),
                    stop=(last and t == PACK - 1),
                )

        def sum_products(w):
            for g in range(HALVES):
                add_transposed(num_t[g], prod_tiles[w], g, w == 0, w == STEPS - 1)

        gate_t = tail.tile([P, A], F32, name="gate_t")
        rec_t = tail.tile([P, A], F32, name="rec_t")
        scale_t = tail.tile([P, A], F32, name="scale_t")

        def gate():
            for g in range(HALVES):
                q_t = single_banks.tile([P, BANK], F32, tag=("turn", "spread")[g], name="q_t")
                for t in range(PACK):
                    c = g * PACK + t
                    nc.tensor.matmul_mx(
                        out=q_t[:, t * B : (t + 1) * B],
                        lhsT=wq_codes[:, c * P : (c + 1) * P].bitcast(FP8X4),
                        lhsT_scale=wq_scales[:, c * P : (c + 1) * P],
                        rhs=zc_codes[:].bitcast(FP8X4),
                        rhs_scale=zc_scales[:],
                        start=True,
                        stop=True,
                    )
                nc.scalar.activation(
                    out=gate_t[:, g * BANK : (g + 1) * BANK], in_=q_t[:], func=ACT.Sigmoid
                )

        den_t = {}

        def turn_denominator():
            for g in range(HALVES):
                den_t[g] = key_banks.tile([P, BANK], F32, tag="keys", name="den_t")
                add_transposed(den_t[g], den, g, True, False)
                add_transposed(den_t[g], e_tiles[STEPS - 1], g, False, True)

        def gate_over_denominator():
            for g in range(HALVES):
                cols = slice(g * BANK, (g + 1) * BANK)
                nc.vector.reciprocal(out=rec_t[:, cols], in_=den_t[g][:])
                nc.vector.tensor_tensor(
                    out=scale_t[:, cols], in0=rec_t[:, cols], in1=gate_t[:, cols], op=ALU.mult
                )

        value_grouped, later_grouped = {}, {}
        for n in range(STEPS + LAG + 1):
            j = n - LAG
            if 2 <= n < STEPS + 2:
                exponentials(n - 2)
            if n < STEPS:
                k_banks[n] = step_matmul(key_banks, "keys", n, wk_codes, wk_scales)
            if n == STEPS + 1:
                gate()
            if 0 <= j < STEPS:
                v_banks[j] = step_matmul(value_banks, "values", j, wv_codes, wv_scales)
            if n < STEPS:
                park_keys(n, 0)
            if 1 <= n <= len(value_groups):
                quantise(value_groups[n - 1], value_grouped[n - 1])
            if 1 <= n <= len(stream) and stream[n - 1][2]:
                quantise(later_groups[stream[n - 1][0]], later_grouped[stream[n - 1][0]])
            if n < STEPS:
                park_keys(n, 1)
            if 1 <= n < STEPS + 1:
                spread_maxima(n - 1)
            if n == STEPS + 2:
                turn_denominator()
            if n < len(value_groups):
                value_grouped[n] = turn_whole(value_groups[n])
            if n < len(stream):
                index, half = stream[n][0], stream[n][1]
                if half == 0:
                    later_grouped[index] = new_grouped()
                turn_half(later_groups[index], later_grouped[index], half, single_banks, "turn")
            if 1 <= j < STEPS + 1:
                sum_products(j - 1)
            if 0 <= j < STEPS:
                products(j)
            if 1 <= n < STEPS + 1:
                step_maximum(n - 1)
            if n == STEPS + 2:
                gate_over_denominator()

        h_grouped = tail.tile([P, HALVES * B * PACK], BF16, name="h_grouped", align_bytes=64)
        h_codes = tail.tile([P, HALVES * B], U32, name="h_codes", align_bytes=64)
        h_scales = tail.tile([P, HALVES * B], U8, name="h_scales", align_bytes=64)
        for g in range(HALVES):
            cols = slice(g * BANK, (g + 1) * BANK)
            nc.vector.tensor_tensor(
                out=h_grouped[:, cols].rearrange("p (b t) -> p b t", t=PACK),
                in0=num_t[g][:].rearrange("p (t b) -> p b t", t=PACK),
                in1=scale_t[:, cols].rearrange("p (t b) -> p b t", t=PACK),
                op=ALU.mult,
            )
        nc.vector.quantize_mx(out=h_codes[:].bitcast(FP8X4), scales=h_scales[:], in_=h_grouped[:])
        out_bank = single_banks.tile([P, BANK], F32, tag="turn")
        for g in range(HALVES):
            nc.tensor.matmul_mx(
                out=out_bank[:],
                lhsT=h_codes[:, g * B : (g + 1) * B].bitcast(FP8X4),
                lhsT_scale=h_scales[:, g * B : (g + 1) * B],
                rhs=wo_codes[:, g * L : (g + 1) * L].bitcast(FP8X4),
                rhs_scale=wo_scales[:, g * L : (g + 1) * L],
                start=(g == 0),
                stop=(g == HALVES - 1),
            )
        result = tail.tile([P, L], F32, name="result")
        nc.scalar.copy(out=result[:], in_=out_bank[:])
        nc.sync.dma_start(out=out, in_=result[:])
